import numpy as np
import ml_dtypes

BF16 = ml_dtypes.bfloat16


def bf(x):
    return np.asarray(x, np.float32).astype(BF16)


def f32(x):
    return np.asarray(x, np.float32)


def f64(x):
    return np.asarray(x).astype(np.float64)


def striped(idx):
    return np.tile(idx.reshape(-1, 16).T, (8, 1))


C, C2, S, P, NH, HEADS, HD, N = 128, 256, 1024, 512, 9, 4, 32, 4608


def unit_columns(a):
    a = a - a.mean(axis=0, keepdims=True)
    return a / np.sqrt((a * a).mean(axis=0, keepdims=True))


def setup_inputs():
    xkv = f32(unit_columns(np.random.standard_normal((C, S))))
    wkv = bf(np.random.standard_normal((C, C2)) / np.sqrt(C))
    bv = f32(0.1 * np.random.standard_normal((C, 1)))
    q = f32(unit_columns(np.random.standard_normal((C, P))))
    idx = np.concatenate([np.random.permutation(S)[:P] for _ in range(NH)])
    return {"xkv": xkv, "wkv": wkv, "bv": bv, "q": q, "offs": striped(idx)}


def reference(xkv, wkv, bv, q, offs):
    idx = offs[:16].T.reshape(-1)
    kv = f64(wkv).T @ f64(xkv)
    kv[C:] += f64(bv)
    prod = kv[:C][:, idx].reshape(C, NH, P) * f64(q)[:, None, :]
    sc = prod.reshape(HEADS, HD, NH, P).sum(axis=1) / np.sqrt(HD)
    e = np.exp(sc)
    attn = e / e.sum(axis=1, keepdims=True)
    a = np.repeat(attn, HD, axis=0)
    return (kv[C:][:, idx].reshape(C, NH, P) * a).sum(axis=1)

@@ -1,0 +1,94 @@
+import math
+
+import concourse.mybir as mybir
+
+F32, BF16, U16 = mybir.dt.float32, mybir.dt.bfloat16, mybir.dt.uint16
+ALU = mybir.AluOpType
+ACT = mybir.ActivationFunctionType
+AXIS = mybir.AxisListType
+
+C = 128
+CELLS = 1024
+QUERIES = 512
+NEIGHBOURS = 9
+HEAD_DIM = 32
+BANK = 512
+PIECE_COLS = QUERIES // 16
+
+FLOPS = 2 * C * (2 * C) * CELLS + 4 * C * NEIGHBOURS * QUERIES
+
+
+def tile_asc_gridcrossattention_kernel(tc, xkv, wkv, bv, q, offs, out):
+    nc = tc.nc
+    with (
+        tc.tile_pool(name="held", bufs=1) as held,
+        tc.tile_pool(name="ring", bufs=3) as ring,
+        tc.psum_pool(name="psum", bufs=2) as psum,
+    ):
+        offsets = held.tile([C, NEIGHBOURS * PIECE_COLS], U16, name="offsets")
+        nc.sync.dma_start(offsets[:], offs)
+        cells_f32 = held.tile([C, CELLS], F32, name="cells_f32")
+        nc.sync.dma_start(cells_f32[:], xkv)
+        weights = held.tile([C, 2 * C], BF16, name="weights")
+        nc.scalar.dma_start(weights[:], wkv)
+        queries = held.tile([C, QUERIES], F32, name="queries")
+        nc.scalar.dma_start(queries[:], q)
+        value_bias = held.tile([C, 1], F32, name="value_bias")
+        nc.scalar.dma_start(value_bias[:], bv)
+
+        head_ones = held.tile([C, C], BF16, name="head_ones")
+        nc.vector.memset(head_ones[:], 0.0)
+        for h in range(C // HEAD_DIM):
+            head = slice(h * HEAD_DIM, (h + 1) * HEAD_DIM)
+            nc.vector.memset(head_ones[head, head], 1.0)
+
+        cells = held.tile([C, CELLS], BF16, name="cells")
+        nc.vector.tensor_copy(cells[:], cells_f32[:])
+        keys = held.tile([C, CELLS], F32, name="keys")
+        values = held.tile([C, CELLS], F32, name="values")
+        for b in range(CELLS // BANK):
+            cols = slice(b * BANK, (b + 1) * BANK)
+            keys_ps = psum.tile([C, BANK], F32, name="keys_ps")
+            nc.tensor.matmul(keys_ps[:], weights[:, 0:C], cells[:, cols], start=True, stop=True)
+            nc.vector.tensor_copy(keys[:, cols], keys_ps[:])
+            values_ps = psum.tile([C, BANK], F32, name="values_ps")
+            nc.tensor.matmul(values_ps[:], weights[:, C : 2 * C], cells[:, cols], start=True, stop=True)
+            nc.scalar.activation(values[:, cols], values_ps[:], ACT.Identity, bias=value_bias[:])
+
+        scores = held.tile([C, NEIGHBOURS, QUERIES], F32, name="scores")
+        for n in range(NEIGHBOURS):
+            piece = offsets[:, n * PIECE_COLS : (n + 1) * PIECE_COLS]
+            prod = ring.tile([C, QUERIES], F32, name="prod")
+            nc.vector.tensor_tensor(prod[:], keys[:].indirect(piece), queries[:], ALU.mult)
+            prod_bf = ring.tile([C, QUERIES], BF16, name="prod_bf")
+            nc.scalar.copy(prod_bf[:], prod[:])
+            scores_ps = psum.tile([C, QUERIES], F32, name="scores_ps")
+            nc.tensor.matmul(scores_ps[:], head_ones[:], prod_bf[:], start=True, stop=True)
+            nc.scalar.copy(scores[:, n, :], scores_ps[:])
+
+        def over_neighbours(tile):
+            return tile[:].rearrange("c n t -> c t n")
+
+        def for_each_neighbour(tile):
+            return tile[:].unsqueeze(1).to_broadcast([C, NEIGHBOURS, QUERIES])
+
+        top = held.tile([C, QUERIES], F32, name="top")
+        nc.vector.tensor_reduce(top[:], over_neighbours(scores), axis=AXIS.X, op=ALU.max)
+        shifted = held.tile([C, NEIGHBOURS, QUERIES], F32, name="shifted")
+        nc.vector.tensor_tensor(shifted[:], scores[:], for_each_neighbour(top), ALU.subtract)
+        expd = held.tile([C, NEIGHBOURS, QUERIES], F32, name="expd")
+        nc.scalar.activation(expd[:], shifted[:], ACT.Exp, scale=1.0 / math.sqrt(HEAD_DIM))
+        total = held.tile([C, QUERIES], F32, name="total")
+        nc.vector.tensor_reduce(total[:], over_neighbours(expd), axis=AXIS.X, op=ALU.add)
+        inverse = held.tile([C, QUERIES], F32, name="inverse")
+        nc.vector.reciprocal(inverse[:], total[:])
+        attn = held.tile([C, NEIGHBOURS, QUERIES], F32, name="attn")
+        nc.vector.tensor_tensor(attn[:], expd[:], for_each_neighbour(inverse), ALU.mult)
+
+        weighted = held.tile([C, NEIGHBOURS, QUERIES], F32, name="weighted")
+        for n in range(NEIGHBOURS):
+            piece = offsets[:, n * PIECE_COLS : (n + 1) * PIECE_COLS]
+            nc.vector.tensor_tensor(weighted[:, n, :], values[:].indirect(piece), attn[:, n, :], ALU.mult)
+        result = held.tile([C, QUERIES], F32, name="result")
+        nc.vector.tensor_reduce(result[:], over_neighbours(weighted), axis=AXIS.X, op=ALU.add)
+        nc.sync.dma_start(out, result[:])

@@ -1,6 +1,7 @@
 import math
 
 import concourse.mybir as mybir
+from concourse.masks import make_identity
 
 F32, BF16, U16 = mybir.dt.float32, mybir.dt.bfloat16, mybir.dt.uint16
 ALU = mybir.AluOpType
@@ -11,9 +12,15 @@ C = 128
 CELLS = 1024
 QUERIES = 512
 NEIGHBOURS = 9
+HEADS = 4
 HEAD_DIM = 32
-BANK = 512
-PIECE_COLS = QUERIES // 16
+HALF = 256
+HALVES = QUERIES // HALF
+BLOCK = 128
+BLOCKS = HALF // BLOCK
+CHUNK = 256
+CHUNKS = CELLS // CHUNK
+SPREAD = 3
 
 FLOPS = 2 * C * (2 * C) * CELLS + 4 * C * NEIGHBOURS * QUERIES
 
@@ -22,73 +29,127 @@ def tile_asc_gridcrossattention_kernel(tc, xkv, wkv, bv, q, offs, out):
     nc = tc.nc
     with (
         tc.tile_pool(name="held", bufs=1) as held,
-        tc.tile_pool(name="ring", bufs=3) as ring,
+        tc.tile_pool(name="stage", bufs=CHUNKS) as stage,
+        tc.tile_pool(name="ring", bufs=4) as ring,
+        tc.tile_pool(name="per_half", bufs=HALVES) as per_half,
         tc.psum_pool(name="psum", bufs=2) as psum,
     ):
-        offsets = held.tile([C, NEIGHBOURS * PIECE_COLS], U16, name="offsets")
-        nc.sync.dma_start(offsets[:], offs)
-        cells_f32 = held.tile([C, CELLS], F32, name="cells_f32")
-        nc.sync.dma_start(cells_f32[:], xkv)
         weights = held.tile([C, 2 * C], BF16, name="weights")
         nc.scalar.dma_start(weights[:], wkv)
+        cells_f32 = []
+        for j in range(CHUNKS):
+            chunk_f32 = stage.tile([C, CHUNK], F32, name="chunk_f32")
+            queue = nc.sync if j % 2 == 0 else nc.scalar
+            queue.dma_start(chunk_f32[:], xkv[:, j * CHUNK : (j + 1) * CHUNK])
+            cells_f32.append(chunk_f32)
+        offsets = held.tile([C, NEIGHBOURS * QUERIES // 16], U16, name="offsets")
+        nc.sync.dma_start(offsets[:], offs)
         queries = held.tile([C, QUERIES], F32, name="queries")
         nc.scalar.dma_start(queries[:], q)
         value_bias = held.tile([C, 1], F32, name="value_bias")
-        nc.scalar.dma_start(value_bias[:], bv)
+        nc.sync.dma_start(value_bias[:], bv)
 
-        head_ones = held.tile([C, C], BF16, name="head_ones")
-        nc.vector.memset(head_ones[:], 0.0)
-        for h in range(C // HEAD_DIM):
-            head = slice(h * HEAD_DIM, (h + 1) * HEAD_DIM)
-            nc.vector.memset(head_ones[head, head], 1.0)
+        head_cols = held.tile([C, HEADS], BF16, name="head_cols")
+        nc.vector.memset(head_cols[:], 0.0)
+        for h in range(HEADS):
+            nc.vector.memset(head_cols[h * HEAD_DIM : (h + 1) * HEAD_DIM, h : h + 1], 1.0)
+        identity = held.tile([C, C], F32, name="identity")
+        make_identity(nc, identity[:])
 
         cells = held.tile([C, CELLS], BF16, name="cells")
-        nc.vector.tensor_copy(cells[:], cells_f32[:])
         keys = held.tile([C, CELLS], F32, name="keys")
         values = held.tile([C, CELLS], F32, name="values")
-        for b in range(CELLS // BANK):
-            cols = slice(b * BANK, (b + 1) * BANK)
-            keys_ps = psum.tile([C, BANK], F32, name="keys_ps")
+        for j in range(CHUNKS):
+            cols = slice(j * CHUNK, (j + 1) * CHUNK)
+            keys_ps = psum.tile([C, CHUNK], F32, name="keys_ps", tag="bank", bufs=4)
+            if j % 2 == 0:
+                nc.vector.tensor_copy(cells[:, cols], cells_f32[j][:])
+            else:
+                nc.scalar.copy(cells[:, cols], cells_f32[j][:])
             nc.tensor.matmul(keys_ps[:], weights[:, 0:C], cells[:, cols], start=True, stop=True)
-            nc.vector.tensor_copy(keys[:, cols], keys_ps[:])
-            values_ps = psum.tile([C, BANK], F32, name="values_ps")
+            if j % 2 == 0:
+                nc.vector.tensor_copy(keys[:, cols], keys_ps[:])
+            else:
+                nc.scalar.copy(keys[:, cols], keys_ps[:])
+        for j in range(CHUNKS):
+            cols = slice(j * CHUNK, (j + 1) * CHUNK)
+            values_ps = psum.tile([C, CHUNK], F32, name="values_ps", tag="bank", bufs=4)
             nc.tensor.matmul(values_ps[:], weights[:, C : 2 * C], cells[:, cols], start=True, stop=True)
             nc.scalar.activation(values[:, cols], values_ps[:], ACT.Identity, bias=value_bias[:])
 
-        scores = held.tile([C, NEIGHBOURS, QUERIES], F32, name="scores")
-        for n in range(NEIGHBOURS):
-            piece = offsets[:, n * PIECE_COLS : (n + 1) * PIECE_COLS]
-            prod = ring.tile([C, QUERIES], F32, name="prod")
-            nc.vector.tensor_tensor(prod[:], keys[:].indirect(piece), queries[:], ALU.mult)
-            prod_bf = ring.tile([C, QUERIES], BF16, name="prod_bf")
-            nc.scalar.copy(prod_bf[:], prod[:])
-            scores_ps = psum.tile([C, QUERIES], F32, name="scores_ps")
-            nc.tensor.matmul(scores_ps[:], head_ones[:], prod_bf[:], start=True, stop=True)
-            nc.scalar.copy(scores[:, n, :], scores_ps[:])
+        def piece(n, half):
+            first = (n * QUERIES + half * HALF) // 16
+            return offsets[:, first : first + HALF // 16]
 
-        def over_neighbours(tile):
-            return tile[:].rearrange("c n t -> c t n")
+        def scores_of(half):
+            scores_ps = psum.tile([BLOCK, NEIGHBOURS, BLOCKS, HEADS], F32, name="scores_ps")
+            for n in range(NEIGHBOURS):
+                prod = ring.tile([C, HALF], F32, name="prod")
+                nc.vector.tensor_tensor(
+                    prod[:], keys[:].indirect(piece(n, half)), queries[:, half * HALF : (half + 1) * HALF], ALU.mult
+                )
+                prod_bf = ring.tile([C, HALF], BF16, name="prod_bf")
+                nc.scalar.copy(prod_bf[:], prod[:])
+                for b in range(BLOCKS):
+                    nc.tensor.matmul(
+                        scores_ps[:, n, b, :], prod_bf[:, b * BLOCK : (b + 1) * BLOCK], head_cols[:], start=True, stop=True
+                    )
+            return scores_ps
 
-        def for_each_neighbour(tile):
-            return tile[:].unsqueeze(1).to_broadcast([C, NEIGHBOURS, QUERIES])
+        def softmax_of(scores_ps):
+            whole = [BLOCK, NEIGHBOURS, BLOCKS, HEADS]
 
-        top = held.tile([C, QUERIES], F32, name="top")
-        nc.vector.tensor_reduce(top[:], over_neighbours(scores), axis=AXIS.X, op=ALU.max)
-        shifted = held.tile([C, NEIGHBOURS, QUERIES], F32, name="shifted")
-        nc.vector.tensor_tensor(shifted[:], scores[:], for_each_neighbour(top), ALU.subtract)
-        expd = held.tile([C, NEIGHBOURS, QUERIES], F32, name="expd")
-        nc.scalar.activation(expd[:], shifted[:], ACT.Exp, scale=1.0 / math.sqrt(HEAD_DIM))
-        total = held.tile([C, QUERIES], F32, name="total")
-        nc.vector.tensor_reduce(total[:], over_neighbours(expd), axis=AXIS.X, op=ALU.add)
-        inverse = held.tile([C, QUERIES], F32, name="inverse")
-        nc.vector.reciprocal(inverse[:], total[:])
-        attn = held.tile([C, NEIGHBOURS, QUERIES], F32, name="attn")
-        nc.vector.tensor_tensor(attn[:], expd[:], for_each_neighbour(inverse), ALU.mult)
+            def neighbours_last(tile):
+                return tile[:].rearrange("t n b h -> t b h n")
 
-        weighted = held.tile([C, NEIGHBOURS, QUERIES], F32, name="weighted")
-        for n in range(NEIGHBOURS):
-            piece = offsets[:, n * PIECE_COLS : (n + 1) * PIECE_COLS]
-            nc.vector.tensor_tensor(weighted[:, n, :], values[:].indirect(piece), attn[:, n, :], ALU.mult)
-        result = held.tile([C, QUERIES], F32, name="result")
-        nc.vector.tensor_reduce(result[:], over_neighbours(weighted), axis=AXIS.X, op=ALU.add)
-        nc.sync.dma_start(out, result[:])
+            def for_each_neighbour(tile):
+                return tile[:].unsqueeze(1).to_broadcast(whole)
+
+            top = per_half.tile([BLOCK, BLOCKS, HEADS], F32, name="top")
+            nc.vector.tensor_reduce(top[:], neighbours_last(scores_ps), axis=AXIS.X, op=ALU.max)
+            shifted = per_half.tile(whole, F32, name="shifted")
+            nc.vector.tensor_tensor(shifted[:], scores_ps[:], for_each_neighbour(top), ALU.subtract)
+            expd = per_half.tile(whole, F32, name="expd")
+            nc.scalar.activation(expd[:], shifted[:], ACT.Exp, scale=1.0 / math.sqrt(HEAD_DIM))
+            total = per_half.tile([BLOCK, BLOCKS, HEADS], F32, name="total")
+            nc.vector.tensor_reduce(total[:], neighbours_last(expd), axis=AXIS.X, op=ALU.add)
+            inverse = per_half.tile([BLOCK, BLOCKS, HEADS], F32, name="inverse")
+            nc.vector.reciprocal(inverse[:], total[:])
+            attn_t = per_half.tile(whole, F32, name="attn_t")
+            nc.vector.tensor_tensor(attn_t[:], expd[:], for_each_neighbour(inverse), ALU.mult)
+            return attn_t
+
+        def spread_of(attn_t):
+            wide = per_half.tile([BLOCK, NEIGHBOURS, BLOCKS, C], F32, name="wide")
+            for n in range(0, NEIGHBOURS, SPREAD):
+                narrow = attn_t[:, n : n + SPREAD, :, :].rearrange("t n b h -> t (n b h)")
+                nc.gpsimd.tensor_copy(
+                    wide[:, n : n + SPREAD, :, :].rearrange("t n b (h l) -> t (n b h) l", l=HEAD_DIM),
+                    narrow.unsqueeze(2).to_broadcast([BLOCK, SPREAD * BLOCKS * HEADS, HEAD_DIM]),
+                )
+            return wide
+
+        def turned_back(wide):
+            attn = per_half.tile([C, NEIGHBOURS, HALF], F32, name="attn")
+            for n in range(NEIGHBOURS):
+                attn_ps = psum.tile([C, HALF], F32, name="attn_ps", tag="bank", bufs=4)
+                for b in range(BLOCKS):
+                    nc.tensor.transpose(attn_ps[:, b * BLOCK : (b + 1) * BLOCK], wide[:, n, b, :], identity[:])
+                nc.scalar.copy(attn[:, n, :], attn_ps[:])
+            return attn
+
+        def output_of(half, attn):
+            out_ps = psum.tile([C, HALF], F32, name="out_ps")
+            for n in range(NEIGHBOURS):
+                weighted = ring.tile([C, HALF], F32, name="weighted")
+                nc.vector.tensor_tensor(weighted[:], values[:].indirect(piece(n, half)), attn[:, n, :], ALU.mult)
+                nc.tensor.matmul(out_ps[:], identity[:], weighted[:], start=(n == 0), stop=(n == NEIGHBOURS - 1))
+            result = per_half.tile([C, HALF], F32, name="result")
+            nc.scalar.copy(result[:], out_ps[:])
+            nc.sync.dma_start(out[:, half * HALF : (half + 1) * HALF], result[:])
+
+        attns = []
+        for half in range(HALVES):
+            attns.append(turned_back(spread_of(softmax_of(scores_of(half)))))
+        for half in range(HALVES):
+            output_of(half, attns[half])

@@ -55,6 +55,8 @@ def tile_asc_gridcrossattention_kernel(tc, xkv, wkv, bv, q, offs, out):
             nc.vector.memset(head_cols[h * HEAD_DIM : (h + 1) * HEAD_DIM, h : h + 1], 1.0)
         identity = held.tile([C, C], F32, name="identity")
         make_identity(nc, identity[:])
+        warm = held.tile([C, HEADS], F32, name="warm")
+        nc.scalar.activation(warm[:], head_cols[:], ACT.Exp)
 
         cells = held.tile([C, CELLS], BF16, name="cells")
         keys = held.tile([C, CELLS], F32, name="keys")
@@ -139,11 +141,27 @@ def tile_asc_gridcrossattention_kernel(tc, xkv, wkv, bv, q, offs, out):
             return attn
 
         def output_of(half, attn):
-            out_ps = psum.tile([C, HALF], F32, name="out_ps")
+            weighted = per_half.tile([C, NEIGHBOURS, HALF], F32, name="weighted")
+            sums_ps = [psum.tile([BLOCK, C], F32, name=f"sum_ps{b}", bufs=1) for b in range(BLOCKS)]
             for n in range(NEIGHBOURS):
-                weighted = ring.tile([C, HALF], F32, name="weighted")
-                nc.vector.tensor_tensor(weighted[:], values[:].indirect(piece(n, half)), attn[:, n, :], ALU.mult)
-                nc.tensor.matmul(out_ps[:], identity[:], weighted[:], start=(n == 0), stop=(n == NEIGHBOURS - 1))
+                nc.vector.tensor_tensor(weighted[:, n, :], values[:].indirect(piece(n, half)), attn[:, n, :], ALU.mult)
+                for b in range(BLOCKS):
+                    nc.tensor.matmul(
+                        sums_ps[b][:],
+                        weighted[:, n, b * BLOCK : (b + 1) * BLOCK],
+                        identity[:],
+                        is_transpose=True,
+                        start=(n == 0),
+                        stop=(n == NEIGHBOURS - 1),
+                    )
+            sums = per_half.tile([BLOCK, BLOCKS, C], F32, name="sums")
+            out_ps = psum.tile([C, HALF], F32, name="out_ps", tag="bank", bufs=4)
+            for b in range(BLOCKS):
+                if b % 2 == 0:
+                    nc.vector.tensor_copy(sums[:, b, :], sums_ps[b][:])
+                else:
+                    nc.scalar.copy(sums[:, b, :], sums_ps[b][:])
+                nc.tensor.transpose(out_ps[:, b * BLOCK : (b + 1) * BLOCK], sums[:, b, :], identity[:])
             result = per_half.tile([C, HALF], F32, name="result")
             nc.scalar.copy(result[:], out_ps[:])
             nc.sync.dma_start(out[:, half * HALF : (half + 1) * HALF], result[:])

@@ -20,7 +20,6 @@ BLOCK = 128
 BLOCKS = HALF // BLOCK
 CHUNK = 256
 CHUNKS = CELLS // CHUNK
-SPREAD = 3
 
 FLOPS = 2 * C * (2 * C) * CELLS + 4 * C * NEIGHBOURS * QUERIES
 
@@ -29,25 +28,23 @@ def tile_asc_gridcrossattention_kernel(tc, xkv, wkv, bv, q, offs, out):
     nc = tc.nc
     with (
         tc.tile_pool(name="held", bufs=1) as held,
-        tc.tile_pool(name="stage", bufs=CHUNKS) as stage,
         tc.tile_pool(name="ring", bufs=4) as ring,
         tc.tile_pool(name="per_half", bufs=HALVES) as per_half,
         tc.psum_pool(name="psum", bufs=2) as psum,
     ):
         weights = held.tile([C, 2 * C], BF16, name="weights")
         nc.scalar.dma_start(weights[:], wkv)
-        cells_f32 = []
+        queries = held.tile([C, QUERIES], F32, name="queries")
+        nc.gpsimd.dma_start(queries[:], q)
+        cells_f32 = held.tile([C, CELLS], F32, name="cells_f32")
         for j in range(CHUNKS):
-            chunk_f32 = stage.tile([C, CHUNK], F32, name="chunk_f32")
+            cols = slice(j * CHUNK, (j + 1) * CHUNK)
             queue = nc.sync if j % 2 == 0 else nc.scalar
-            queue.dma_start(chunk_f32[:], xkv[:, j * CHUNK : (j + 1) * CHUNK])
-            cells_f32.append(chunk_f32)
+            queue.dma_start(cells_f32[:, cols], xkv[:, cols])
         offsets = held.tile([C, NEIGHBOURS * QUERIES // 16], U16, name="offsets")
         nc.sync.dma_start(offsets[:], offs)
-        queries = held.tile([C, QUERIES], F32, name="queries")
-        nc.scalar.dma_start(queries[:], q)
         value_bias = held.tile([C, 1], F32, name="value_bias")
-        nc.sync.dma_start(value_bias[:], bv)
+        nc.gpsimd.dma_start(value_bias[:], bv)
 
         head_cols = held.tile([C, HEADS], BF16, name="head_cols")
         nc.vector.memset(head_cols[:], 0.0)
@@ -65,9 +62,9 @@ def tile_asc_gridcrossattention_kernel(tc, xkv, wkv, bv, q, offs, out):
             cols = slice(j * CHUNK, (j + 1) * CHUNK)
             keys_ps = psum.tile([C, CHUNK], F32, name="keys_ps", tag="bank", bufs=4)
             if j % 2 == 0:
-                nc.vector.tensor_copy(cells[:, cols], cells_f32[j][:])
+                nc.vector.tensor_copy(cells[:, cols], cells_f32[:, cols])
             else:
-                nc.scalar.copy(cells[:, cols], cells_f32[j][:])
+                nc.scalar.copy(cells[:, cols], cells_f32[:, cols])
             nc.tensor.matmul(keys_ps[:], weights[:, 0:C], cells[:, cols], start=True, stop=True)
             if j % 2 == 0:
                 nc.vector.tensor_copy(keys[:, cols], keys_ps[:])
@@ -121,19 +118,17 @@ def tile_asc_gridcrossattention_kernel(tc, xkv, wkv, bv, q, offs, out):
             nc.vector.tensor_tensor(attn_t[:], expd[:], for_each_neighbour(inverse), ALU.mult)
             return attn_t
 
-        def spread_of(attn_t):
+        def turned_back(attn_t):
             wide = per_half.tile([BLOCK, NEIGHBOURS, BLOCKS, C], F32, name="wide")
-            for n in range(0, NEIGHBOURS, SPREAD):
-                narrow = attn_t[:, n : n + SPREAD, :, :].rearrange("t n b h -> t (n b h)")
-                nc.gpsimd.tensor_copy(
-                    wide[:, n : n + SPREAD, :, :].rearrange("t n b (h l) -> t (n b h) l", l=HEAD_DIM),
-                    narrow.unsqueeze(2).to_broadcast([BLOCK, SPREAD * BLOCKS * HEADS, HEAD_DIM]),
-                )
-            return wide
-
-        def turned_back(wide):
             attn = per_half.tile([C, NEIGHBOURS, HALF], F32, name="attn")
             for n in range(NEIGHBOURS):
+                nc.gpsimd.tensor_copy(
+                    wide[:, n, :, :].rearrange("t b (h l) -> t (b h) l", l=HEAD_DIM),
+                    attn_t[:, n, :, :]
+                    .rearrange("t b h -> t (b h)")
+                    .unsqueeze(2)
+                    .to_broadcast([BLOCK, BLOCKS * HEADS, HEAD_DIM]),
+                )
                 attn_ps = psum.tile([C, HALF], F32, name="attn_ps", tag="bank", bufs=4)
                 for b in range(BLOCKS):
                     nc.tensor.transpose(attn_ps[:, b * BLOCK : (b + 1) * BLOCK], wide[:, n, b, :], identity[:])
@@ -157,10 +152,7 @@ def tile_asc_gridcrossattention_kernel(tc, xkv, wkv, bv, q, offs, out):
             sums = per_half.tile([BLOCK, BLOCKS, C], F32, name="sums")
             out_ps = psum.tile([C, HALF], F32, name="out_ps", tag="bank", bufs=4)
             for b in range(BLOCKS):
-                if b % 2 == 0:
-                    nc.vector.tensor_copy(sums[:, b, :], sums_ps[b][:])
-                else:
-                    nc.scalar.copy(sums[:, b, :], sums_ps[b][:])
+                nc.scalar.copy(sums[:, b, :], sums_ps[b][:])
                 nc.tensor.transpose(out_ps[:, b * BLOCK : (b + 1) * BLOCK], sums[:, b, :], identity[:])
             result = per_half.tile([C, HALF], F32, name="result")
             nc.scalar.copy(result[:], out_ps[:])
@@ -168,6 +160,6 @@ def tile_asc_gridcrossattention_kernel(tc, xkv, wkv, bv, q, offs, out):
 
         attns = []
         for half in range(HALVES):
-            attns.append(turned_back(spread_of(softmax_of(scores_of(half)))))
+            attns.append(turned_back(softmax_of(scores_of(half))))
         for half in range(HALVES):
             output_of(half, attns[half])

@@ -20,6 +20,7 @@ BLOCK = 128
 BLOCKS = HALF // BLOCK
 CHUNK = 256
 CHUNKS = CELLS // CHUNK
+SPREAD = 3
 
 FLOPS = 2 * C * (2 * C) * CELLS + 4 * C * NEIGHBOURS * QUERIES
 
@@ -34,8 +35,6 @@ def tile_asc_gridcrossattention_kernel(tc, xkv, wkv, bv, q, offs, out):
     ):
         weights = held.tile([C, 2 * C], BF16, name="weights")
         nc.scalar.dma_start(weights[:], wkv)
-        queries = held.tile([C, QUERIES], F32, name="queries")
-        nc.gpsimd.dma_start(queries[:], q)
         cells_f32 = held.tile([C, CELLS], F32, name="cells_f32")
         for j in range(CHUNKS):
             cols = slice(j * CHUNK, (j + 1) * CHUNK)
@@ -43,8 +42,10 @@ def tile_asc_gridcrossattention_kernel(tc, xkv, wkv, bv, q, offs, out):
             queue.dma_start(cells_f32[:, cols], xkv[:, cols])
         offsets = held.tile([C, NEIGHBOURS * QUERIES // 16], U16, name="offsets")
         nc.sync.dma_start(offsets[:], offs)
+        queries = held.tile([C, QUERIES], F32, name="queries")
+        nc.scalar.dma_start(queries[:], q)
         value_bias = held.tile([C, 1], F32, name="value_bias")
-        nc.gpsimd.dma_start(value_bias[:], bv)
+        nc.sync.dma_start(value_bias[:], bv)
 
         head_cols = held.tile([C, HEADS], BF16, name="head_cols")
         nc.vector.memset(head_cols[:], 0.0)
@@ -121,18 +122,19 @@ def tile_asc_gridcrossattention_kernel(tc, xkv, wkv, bv, q, offs, out):
         def turned_back(attn_t):
             wide = per_half.tile([BLOCK, NEIGHBOURS, BLOCKS, C], F32, name="wide")
             attn = per_half.tile([C, NEIGHBOURS, HALF], F32, name="attn")
-            for n in range(NEIGHBOURS):
+            for first in range(0, NEIGHBOURS, SPREAD):
                 nc.gpsimd.tensor_copy(
-                    wide[:, n, :, :].rearrange("t b (h l) -> t (b h) l", l=HEAD_DIM),
-                    attn_t[:, n, :, :]
-                    .rearrange("t b h -> t (b h)")
+                    wide[:, first : first + SPREAD, :, :].rearrange("t n b (h l) -> t (n b h) l", l=HEAD_DIM),
+                    attn_t[:, first : first + SPREAD, :, :]
+                    .rearrange("t n b h -> t (n b h)")
                     .unsqueeze(2)
-                    .to_broadcast([BLOCK, BLOCKS * HEADS, HEAD_DIM]),
+                    .to_broadcast([BLOCK, SPREAD * BLOCKS * HEADS, HEAD_DIM]),
                 )
-                attn_ps = psum.tile([C, HALF], F32, name="attn_ps", tag="bank", bufs=4)
-                for b in range(BLOCKS):
-                    nc.tensor.transpose(attn_ps[:, b * BLOCK : (b + 1) * BLOCK], wide[:, n, b, :], identity[:])
-                nc.scalar.copy(attn[:, n, :], attn_ps[:])
+                for n in range(first, first + SPREAD):
+                    attn_ps = psum.tile([C, HALF], F32, name="attn_ps", tag="bank", bufs=4)
+                    for b in range(BLOCKS):
+                        nc.tensor.transpose(attn_ps[:, b * BLOCK : (b + 1) * BLOCK], wide[:, n, b, :], identity[:])
+                    nc.scalar.copy(attn[:, n, :], attn_ps[:])
             return attn
 
         def output_of(half, attn):

@@ -123,7 +123,7 @@ def tile_asc_gridcrossattention_kernel(tc, xkv, wkv, bv, q, offs, out):
             wide = per_half.tile([BLOCK, NEIGHBOURS, BLOCKS, C], F32, name="wide")
             attn = per_half.tile([C, NEIGHBOURS, HALF], F32, name="attn")
             for first in range(0, NEIGHBOURS, SPREAD):
-                nc.gpsimd.tensor_copy(
+                nc.scalar.copy(
                     wide[:, first : first + SPREAD, :, :].rearrange("t n b (h l) -> t (n b h) l", l=HEAD_DIM),
                     attn_t[:, first : first + SPREAD, :, :]
                     .rearrange("t n b h -> t (n b h)")

@@ -119,11 +119,11 @@ def tile_asc_gridcrossattention_kernel(tc, xkv, wkv, bv, q, offs, out):
             nc.vector.tensor_tensor(attn_t[:], expd[:], for_each_neighbour(inverse), ALU.mult)
             return attn_t
 
-        def turned_back(attn_t):
+        def turned_back(attn_t, spread):
             wide = per_half.tile([BLOCK, NEIGHBOURS, BLOCKS, C], F32, name="wide")
             attn = per_half.tile([C, NEIGHBOURS, HALF], F32, name="attn")
             for first in range(0, NEIGHBOURS, SPREAD):
-                nc.scalar.copy(
+                spread(
                     wide[:, first : first + SPREAD, :, :].rearrange("t n b (h l) -> t (n b h) l", l=HEAD_DIM),
                     attn_t[:, first : first + SPREAD, :, :]
                     .rearrange("t n b h -> t (n b h)")
@@ -160,8 +160,9 @@ def tile_asc_gridcrossattention_kernel(tc, xkv, wkv, bv, q, offs, out):
             nc.scalar.copy(result[:], out_ps[:])
             nc.sync.dma_start(out[:, half * HALF : (half + 1) * HALF], result[:])
 
+        spreads = [nc.vector.tensor_copy, nc.scalar.copy]
         attns = []
         for half in range(HALVES):
-            attns.append(turned_back(softmax_of(scores_of(half))))
+            attns.append(turned_back(softmax_of(scores_of(half)), spreads[half]))
         for half in range(HALVES):
             output_of(half, attns[half])

@@ -18,8 +18,9 @@ HALF = 256
 HALVES = QUERIES // HALF
 BLOCK = 128
 BLOCKS = HALF // BLOCK
-CHUNK = 256
-CHUNKS = CELLS // CHUNK
+CHUNK_WIDTHS = [256, 256, 256, 128, 128]
+CHUNKS = [slice(sum(CHUNK_WIDTHS[:j]), sum(CHUNK_WIDTHS[: j + 1])) for j in range(len(CHUNK_WIDTHS))]
+WIDE = max(CHUNK_WIDTHS)
 SPREAD = 3
 
 FLOPS = 2 * C * (2 * C) * CELLS + 4 * C * NEIGHBOURS * QUERIES
@@ -36,46 +37,44 @@ def tile_asc_gridcrossattention_kernel(tc, xkv, wkv, bv, q, offs, out):
         weights = held.tile([C, 2 * C], BF16, name="weights")
         nc.scalar.dma_start(weights[:], wkv)
         cells_f32 = held.tile([C, CELLS], F32, name="cells_f32")
-        for j in range(CHUNKS):
-            cols = slice(j * CHUNK, (j + 1) * CHUNK)
+        for j, cols in enumerate(CHUNKS):
             queue = nc.sync if j % 2 == 0 else nc.scalar
             queue.dma_start(cells_f32[:, cols], xkv[:, cols])
         offsets = held.tile([C, NEIGHBOURS * QUERIES // 16], U16, name="offsets")
         nc.sync.dma_start(offsets[:], offs)
         queries = held.tile([C, QUERIES], F32, name="queries")
-        nc.scalar.dma_start(queries[:], q)
+        for half in range(HALVES):
+            cols = slice(half * HALF, (half + 1) * HALF)
+            nc.sync.dma_start(queries[:, cols], q[:, cols])
         value_bias = held.tile([C, 1], F32, name="value_bias")
         nc.sync.dma_start(value_bias[:], bv)
 
+        warm = held.tile([C, 1], F32, name="warm")
+        nc.gpsimd.memset(warm[:], 0.0)
+        warmed = held.tile([C, 1], F32, name="warmed")
+        nc.scalar.activation(warmed[:], warm[:], ACT.Exp)
         head_cols = held.tile([C, HEADS], BF16, name="head_cols")
         nc.vector.memset(head_cols[:], 0.0)
         for h in range(HEADS):
             nc.vector.memset(head_cols[h * HEAD_DIM : (h + 1) * HEAD_DIM, h : h + 1], 1.0)
         identity = held.tile([C, C], F32, name="identity")
         make_identity(nc, identity[:])
-        warm = held.tile([C, HEADS], F32, name="warm")
-        nc.scalar.activation(warm[:], head_cols[:], ACT.Exp)
 
         cells = held.tile([C, CELLS], BF16, name="cells")
         keys = held.tile([C, CELLS], F32, name="keys")
         values = held.tile([C, CELLS], F32, name="values")
-        for j in range(CHUNKS):
-            cols = slice(j * CHUNK, (j + 1) * CHUNK)
-            keys_ps = psum.tile([C, CHUNK], F32, name="keys_ps", tag="bank", bufs=4)
-            if j % 2 == 0:
-                nc.vector.tensor_copy(cells[:, cols], cells_f32[:, cols])
+        for cols, width in zip(CHUNKS, CHUNK_WIDTHS):
+            keys_ps = psum.tile([C, WIDE], F32, name="keys_ps", tag="bank", bufs=4)
+            nc.vector.tensor_copy(cells[:, cols], cells_f32[:, cols])
+            nc.tensor.matmul(keys_ps[:, 0:width], weights[:, 0:C], cells[:, cols], start=True, stop=True)
+            if width < WIDE:
+                nc.vector.tensor_copy(keys[:, cols], keys_ps[:, 0:width])
             else:
-                nc.scalar.copy(cells[:, cols], cells_f32[:, cols])
-            nc.tensor.matmul(keys_ps[:], weights[:, 0:C], cells[:, cols], start=True, stop=True)
-            if j % 2 == 0:
-                nc.vector.tensor_copy(keys[:, cols], keys_ps[:])
-            else:
-                nc.scalar.copy(keys[:, cols], keys_ps[:])
-        for j in range(CHUNKS):
-            cols = slice(j * CHUNK, (j + 1) * CHUNK)
-            values_ps = psum.tile([C, CHUNK], F32, name="values_ps", tag="bank", bufs=4)
-            nc.tensor.matmul(values_ps[:], weights[:, C : 2 * C], cells[:, cols], start=True, stop=True)
-            nc.scalar.activation(values[:, cols], values_ps[:], ACT.Identity, bias=value_bias[:])
+                nc.scalar.copy(keys[:, cols], keys_ps[:, 0:width])
+        for cols, width in zip(CHUNKS, CHUNK_WIDTHS):
+            values_ps = psum.tile([C, WIDE], F32, name="values_ps", tag="bank", bufs=4)
+            nc.tensor.matmul(values_ps[:, 0:width], weights[:, C : 2 * C], cells[:, cols], start=True, stop=True)
+            nc.scalar.activation(values[:, cols], values_ps[:, 0:width], ACT.Identity, bias=value_bias[:])
 
         def piece(n, half):
             first = (n * QUERIES + half * HALF) // 16
@@ -137,11 +136,13 @@ def tile_asc_gridcrossattention_kernel(tc, xkv, wkv, bv, q, offs, out):
                     nc.scalar.copy(attn[:, n, :], attn_ps[:])
             return attn
 
-        def output_of(half, attn):
+        def output_of(half, attn, vector_closes):
             weighted = per_half.tile([C, NEIGHBOURS, HALF], F32, name="weighted")
             sums_ps = [psum.tile([BLOCK, C], F32, name=f"sum_ps{b}", bufs=1) for b in range(BLOCKS)]
+            summed_in_psum = NEIGHBOURS - 2 if vector_closes else NEIGHBOURS
             for n in range(NEIGHBOURS):
                 nc.vector.tensor_tensor(weighted[:, n, :], values[:].indirect(piece(n, half)), attn[:, n, :], ALU.mult)
+            for n in range(summed_in_psum):
                 for b in range(BLOCKS):
                     nc.tensor.matmul(
                         sums_ps[b][:],
@@ -149,7 +150,7 @@ def tile_asc_gridcrossattention_kernel(tc, xkv, wkv, bv, q, offs, out):
                         identity[:],
                         is_transpose=True,
                         start=(n == 0),
-                        stop=(n == NEIGHBOURS - 1),
+                        stop=(n == summed_in_psum - 1),
                     )
             sums = per_half.tile([BLOCK, BLOCKS, C], F32, name="sums")
             out_ps = psum.tile([C, HALF], F32, name="out_ps", tag="bank", bufs=4)
@@ -157,7 +158,12 @@ def tile_asc_gridcrossattention_kernel(tc, xkv, wkv, bv, q, offs, out):
                 nc.scalar.copy(sums[:, b, :], sums_ps[b][:])
                 nc.tensor.transpose(out_ps[:, b * BLOCK : (b + 1) * BLOCK], sums[:, b, :], identity[:])
             result = per_half.tile([C, HALF], F32, name="result")
-            nc.scalar.copy(result[:], out_ps[:])
+            if vector_closes:
+                last_two = per_half.tile([C, HALF], F32, name="last_two")
+                nc.vector.tensor_tensor(last_two[:], weighted[:, NEIGHBOURS - 2, :], weighted[:, NEIGHBOURS - 1, :], ALU.add)
+                nc.vector.tensor_tensor(result[:], out_ps[:], last_two[:], ALU.add)
+            else:
+                nc.scalar.copy(result[:], out_ps[:])
             nc.sync.dma_start(out[:, half * HALF : (half + 1) * HALF], result[:])
 
         spreads = [nc.vector.tensor_copy, nc.scalar.copy]
@@ -165,4 +171,4 @@ def tile_asc_gridcrossattention_kernel(tc, xkv, wkv, bv, q, offs, out):
         for half in range(HALVES):
             attns.append(turned_back(softmax_of(scores_of(half)), spreads[half]))
         for half in range(HALVES):
-            output_of(half, attns[half])
+            output_of(half, attns[half], vector_closes=(half == HALVES - 1))

@@ -15,13 +15,14 @@ NEIGHBOURS = 9
 HEADS = 4
 HEAD_DIM = 32
 HALF = 256
+PLACES = 3
+AHEAD = 2
 HALVES = QUERIES // HALF
 BLOCK = 128
 BLOCKS = HALF // BLOCK
 CHUNK_WIDTHS = [256, 256, 256, 128, 128]
 CHUNKS = [slice(sum(CHUNK_WIDTHS[:j]), sum(CHUNK_WIDTHS[: j + 1])) for j in range(len(CHUNK_WIDTHS))]
 WIDE = max(CHUNK_WIDTHS)
-SPREAD = 3
 
 FLOPS = 2 * C * (2 * C) * CELLS + 4 * C * NEIGHBOURS * QUERIES
 
@@ -64,7 +65,7 @@ def tile_asc_gridcrossattention_kernel(tc, xkv, wkv, bv, q, offs, out):
         keys = held.tile([C, CELLS], F32, name="keys")
         values = held.tile([C, CELLS], F32, name="values")
         for cols, width in zip(CHUNKS, CHUNK_WIDTHS):
-            keys_ps = psum.tile([C, WIDE], F32, name="keys_ps", tag="bank", bufs=4)
+            keys_ps = psum.tile([C, WIDE], F32, name="keys_ps", tag="bank", bufs=5)
             nc.vector.tensor_copy(cells[:, cols], cells_f32[:, cols])
             nc.tensor.matmul(keys_ps[:, 0:width], weights[:, 0:C], cells[:, cols], start=True, stop=True)
             if width < WIDE:
@@ -72,7 +73,7 @@ def tile_asc_gridcrossattention_kernel(tc, xkv, wkv, bv, q, offs, out):
             else:
                 nc.scalar.copy(keys[:, cols], keys_ps[:, 0:width])
         for cols, width in zip(CHUNKS, CHUNK_WIDTHS):
-            values_ps = psum.tile([C, WIDE], F32, name="values_ps", tag="bank", bufs=4)
+            values_ps = psum.tile([C, WIDE], F32, name="values_ps", tag="bank", bufs=5)
             nc.tensor.matmul(values_ps[:, 0:width], weights[:, C : 2 * C], cells[:, cols], start=True, stop=True)
             nc.scalar.activation(values[:, cols], values_ps[:, 0:width], ACT.Identity, bias=value_bias[:])
 
@@ -80,80 +81,109 @@ def tile_asc_gridcrossattention_kernel(tc, xkv, wkv, bv, q, offs, out):
             first = (n * QUERIES + half * HALF) // 16
             return offsets[:, first : first + HALF // 16]
 
-        def scores_of(half):
-            scores_ps = psum.tile([BLOCK, NEIGHBOURS, BLOCKS, HEADS], F32, name="scores_ps")
-            for n in range(NEIGHBOURS):
-                prod = ring.tile([C, HALF], F32, name="prod")
-                nc.vector.tensor_tensor(
-                    prod[:], keys[:].indirect(piece(n, half)), queries[:, half * HALF : (half + 1) * HALF], ALU.mult
-                )
-                prod_bf = ring.tile([C, HALF], BF16, name="prod_bf")
-                nc.scalar.copy(prod_bf[:], prod[:])
-                for b in range(BLOCKS):
-                    nc.tensor.matmul(
-                        scores_ps[:, n, b, :], prod_bf[:, b * BLOCK : (b + 1) * BLOCK], head_cols[:], start=True, stop=True
-                    )
-            return scores_ps
+        products = [held.tile([C, NEIGHBOURS, HALF], F32, name=f"products{half}") for half in range(HALVES)]
+        stores = [held.tile([C, 2 * NEIGHBOURS, HALF], F32, name=f"store{half}") for half in range(HALVES)]
+        staged = held.tile([C, PLACES, HALF], F32, name="staged")
+        taken = []
 
-        def softmax_of(scores_ps):
+        def next_place():
+            taken.append(len(taken) % PLACES)
+            return staged[:, taken[-1], :]
+
+        def across(places, n, width):
+            border = (n + 1) * HALF
+            return places.rearrange("c n t -> c (n t)")[:, border - width // 2 : border + width // 2]
+
+        def across_twice(places, n):
+            border = (n + 1) * HALF
+            run = places.rearrange("c n t -> c (n t)")[:, border - BLOCK // 4 : border - BLOCK // 4 + 2 * BLOCKS * HALF]
+            return run.rearrange("c (b t) -> c b t", b=BLOCKS)[:, :, 0 : BLOCK // 2].bitcast(BF16)
+
+        besides = [products[1][:], stores[0][:, NEIGHBOURS:, :]]
+
+        def new_scores():
+            return psum.tile([BLOCK, NEIGHBOURS, BLOCKS, HEADS], F32, name="scores_ps", bufs=1)
+
+        def score(half, n, scores_ps):
+            prod = products[half][:, n, :]
+            nc.vector.tensor_tensor(
+                prod, keys[:].indirect(piece(n, half)), queries[:, half * HALF : (half + 1) * HALF], ALU.mult
+            )
+            if n < NEIGHBOURS - 1:
+                prod_bf = next_place()[:, HALF // 2 : HALF].rearrange("c (b t) -> c b t", b=BLOCKS).bitcast(BF16)
+            else:
+                prod_bf = across_twice(besides[half], 2)
+            nc.scalar.copy(prod_bf, prod.rearrange("c (b t) -> c b t", b=BLOCKS))
+            for b in reversed(range(BLOCKS)):
+                nc.tensor.matmul(scores_ps[:, n, b, :], prod_bf[:, b, :], head_cols[:], start=True, stop=True)
+
+        def softmax_of(scores_ps, beside, top):
             whole = [BLOCK, NEIGHBOURS, BLOCKS, HEADS]
 
-            def neighbours_last(tile):
-                return tile[:].rearrange("t n b h -> t b h n")
+            def neighbours_last(values):
+                return values.rearrange("t n b h -> t b h n")
 
-            def for_each_neighbour(tile):
-                return tile[:].unsqueeze(1).to_broadcast(whole)
+            def small(n):
+                return beside[:, n, 0 : BLOCKS * HEADS].rearrange("t (b h) -> t b h", h=HEADS)
 
-            top = per_half.tile([BLOCK, BLOCKS, HEADS], F32, name="top")
-            nc.vector.tensor_reduce(top[:], neighbours_last(scores_ps), axis=AXIS.X, op=ALU.max)
-            shifted = per_half.tile(whole, F32, name="shifted")
-            nc.vector.tensor_tensor(shifted[:], scores_ps[:], for_each_neighbour(top), ALU.subtract)
-            expd = per_half.tile(whole, F32, name="expd")
-            nc.scalar.activation(expd[:], shifted[:], ACT.Exp, scale=1.0 / math.sqrt(HEAD_DIM))
-            total = per_half.tile([BLOCK, BLOCKS, HEADS], F32, name="total")
-            nc.vector.tensor_reduce(total[:], neighbours_last(expd), axis=AXIS.X, op=ALU.add)
+            def large(n):
+                return across(beside, n, NEIGHBOURS * BLOCKS * HEADS).rearrange("t (n b h) -> t n b h", b=BLOCKS, h=HEADS)
+
+            def for_each_neighbour(values_bh):
+                return values_bh.unsqueeze(1).to_broadcast(whole)
+
+            shifted, total, expd = large(4), small(6), large(7)
             inverse = per_half.tile([BLOCK, BLOCKS, HEADS], F32, name="inverse")
-            nc.vector.reciprocal(inverse[:], total[:])
+            nc.vector.tensor_reduce(top, neighbours_last(scores_ps[:]), axis=AXIS.X, op=ALU.max)
+            nc.vector.tensor_tensor(shifted, scores_ps[:], for_each_neighbour(top), ALU.subtract)
+            nc.scalar.activation(expd, shifted, ACT.Exp, scale=1.0 / math.sqrt(HEAD_DIM))
+            nc.vector.tensor_reduce(total, neighbours_last(expd), axis=AXIS.X, op=ALU.add)
+            nc.vector.reciprocal(inverse[:], total)
             attn_t = per_half.tile(whole, F32, name="attn_t")
-            nc.vector.tensor_tensor(attn_t[:], expd[:], for_each_neighbour(inverse), ALU.mult)
+            nc.vector.tensor_tensor(attn_t[:], expd, for_each_neighbour(inverse[:]), ALU.mult)
             return attn_t
 
-        def turned_back(attn_t, spread):
-            wide = per_half.tile([BLOCK, NEIGHBOURS, BLOCKS, C], F32, name="wide")
-            attn = per_half.tile([C, NEIGHBOURS, HALF], F32, name="attn")
-            for first in range(0, NEIGHBOURS, SPREAD):
-                spread(
-                    wide[:, first : first + SPREAD, :, :].rearrange("t n b (h l) -> t (n b h) l", l=HEAD_DIM),
-                    attn_t[:, first : first + SPREAD, :, :]
-                    .rearrange("t n b h -> t (n b h)")
-                    .unsqueeze(2)
-                    .to_broadcast([BLOCK, SPREAD * BLOCKS * HEADS, HEAD_DIM]),
-                )
-                for n in range(first, first + SPREAD):
-                    attn_ps = psum.tile([C, HALF], F32, name="attn_ps", tag="bank", bufs=4)
-                    for b in range(BLOCKS):
-                        nc.tensor.transpose(attn_ps[:, b * BLOCK : (b + 1) * BLOCK], wide[:, n, b, :], identity[:])
-                    nc.scalar.copy(attn[:, n, :], attn_ps[:])
-            return attn
+        turned = {}
 
-        def output_of(half, attn, vector_closes):
-            weighted = per_half.tile([C, NEIGHBOURS, HALF], F32, name="weighted")
-            sums_ps = [psum.tile([BLOCK, C], F32, name=f"sum_ps{b}", bufs=1) for b in range(BLOCKS)]
-            summed_in_psum = NEIGHBOURS - 2 if vector_closes else NEIGHBOURS
-            for n in range(NEIGHBOURS):
-                nc.vector.tensor_tensor(weighted[:, n, :], values[:].indirect(piece(n, half)), attn[:, n, :], ALU.mult)
-            for n in range(summed_in_psum):
-                for b in range(BLOCKS):
-                    nc.tensor.matmul(
-                        sums_ps[b][:],
-                        weighted[:, n, b * BLOCK : (b + 1) * BLOCK],
-                        identity[:],
-                        is_transpose=True,
-                        start=(n == 0),
-                        stop=(n == summed_in_psum - 1),
-                    )
+        def turn(half, n, attn_t):
+            wide = next_place()
+            nc.scalar.copy(
+                wide.rearrange("t (b h l) -> t (b h) l", b=BLOCKS, l=HEAD_DIM),
+                attn_t[:, n, :, :]
+                .rearrange("t b h -> t (b h)")
+                .unsqueeze(2)
+                .to_broadcast([BLOCK, BLOCKS * HEADS, HEAD_DIM]),
+            )
+            attn_ps = psum.tile([C, HALF], F32, name="attn_ps", tag="bank", bufs=5)
+            for b in range(BLOCKS):
+                block = slice(b * BLOCK, (b + 1) * BLOCK)
+                nc.tensor.transpose(attn_ps[:, block], wide[:, block], identity[:])
+            turned[half, n] = attn_ps
+
+        def weigh(half, n):
+            attn = stores[half][:, n, :]
+            bring = nc.vector.tensor_copy if (half, n) == (0, 0) else nc.scalar.copy
+            bring(attn, turned[half, n][:])
+            nc.vector.tensor_tensor(stores[half][:, NEIGHBOURS + n, :], values[:].indirect(piece(n, half)), attn, ALU.mult)
+
+        def add_up(half, n, sums_ps, last):
+            for b in range(BLOCKS):
+                nc.tensor.matmul(
+                    sums_ps[b][:],
+                    stores[half][:, NEIGHBOURS + n, b * BLOCK : (b + 1) * BLOCK],
+                    identity[:],
+                    is_transpose=True,
+                    start=(n == 0),
+                    stop=(n == last),
+                )
+
+        def new_sums():
+            return [psum.tile([BLOCK, C], F32, name=f"sum_ps{b}", bufs=1) for b in range(BLOCKS)]
+
+        def finish(half, sums_ps, vector_closes):
+            weighted = stores[half][:, NEIGHBOURS:, :]
             sums = per_half.tile([BLOCK, BLOCKS, C], F32, name="sums")
-            out_ps = psum.tile([C, HALF], F32, name="out_ps", tag="bank", bufs=4)
+            out_ps = psum.tile([C, HALF], F32, name="out_ps", tag="bank", bufs=5)
             for b in range(BLOCKS):
                 nc.scalar.copy(sums[:, b, :], sums_ps[b][:])
                 nc.tensor.transpose(out_ps[:, b * BLOCK : (b + 1) * BLOCK], sums[:, b, :], identity[:])
@@ -166,9 +196,44 @@ def tile_asc_gridcrossattention_kernel(tc, xkv, wkv, bv, q, offs, out):
                 nc.scalar.copy(result[:], out_ps[:])
             nc.sync.dma_start(out[:, half * HALF : (half + 1) * HALF], result[:])
 
-        spreads = [nc.vector.tensor_copy, nc.scalar.copy]
-        attns = []
-        for half in range(HALVES):
-            attns.append(turned_back(softmax_of(scores_of(half)), spreads[half]))
-        for half in range(HALVES):
-            output_of(half, attns[half], vector_closes=(half == HALVES - 1))
+        tops = [
+            held.tile([BLOCK, BLOCKS * HEADS], F32, name="top")[:, 0 : BLOCKS * HEADS],
+            stores[0][:, 0, 0 : BLOCKS * HEADS],
+        ]
+        tops = [top.rearrange("t (b h) -> t b h", h=HEADS) for top in tops]
+        last = NEIGHBOURS - 1
+        scores_0 = new_scores()
+        for n in range(NEIGHBOURS):
+            score(0, n, scores_0)
+        attn_0 = softmax_of(scores_0, besides[0], tops[0])
+        scores_1 = new_scores()
+        for n in range(NEIGHBOURS - AHEAD - 1):
+            score(1, n, scores_1)
+        for n in range(AHEAD):
+            turn(0, n, attn_0)
+        score(1, NEIGHBOURS - AHEAD - 1, scores_1)
+        sums_0 = new_sums()
+        for n in range(AHEAD):
+            weigh(0, n)
+            score(1, NEIGHBOURS - AHEAD + n, scores_1)
+            turn(0, AHEAD + n, attn_0)
+        attn_1 = softmax_of(scores_1, besides[1], tops[1])
+        for n in range(AHEAD, NEIGHBOURS):
+            weigh(0, n)
+            if n + AHEAD < NEIGHBOURS:
+                turn(0, n + AHEAD, attn_0)
+            add_up(0, n - AHEAD, sums_0, last)
+        for n in range(AHEAD):
+            turn(1, n, attn_1)
+        for n in range(AHEAD):
+            weigh(1, n)
+            turn(1, n + AHEAD, attn_1)
+            add_up(0, NEIGHBOURS - AHEAD + n, sums_0, last)
+        finish(0, sums_0, vector_closes=False)
+        sums_1 = new_sums()
+        for n in range(AHEAD, NEIGHBOURS):
+            weigh(1, n)
+            if n + AHEAD < NEIGHBOURS:
+                turn(1, n + AHEAD, attn_1)
+            add_up(1, n - AHEAD, sums_1, last - 2)
+        finish(1, sums_1, vector_closes=True)

@@ -65,7 +65,7 @@ def tile_asc_gridcrossattention_kernel(tc, xkv, wkv, bv, q, offs, out):
         keys = held.tile([C, CELLS], F32, name="keys")
         values = held.tile([C, CELLS], F32, name="values")
         for cols, width in zip(CHUNKS, CHUNK_WIDTHS):
-            keys_ps = psum.tile([C, WIDE], F32, name="keys_ps", tag="bank", bufs=5)
+            keys_ps = psum.tile([C, WIDE], F32, name="keys_ps", tag="bank", bufs=7)
             nc.vector.tensor_copy(cells[:, cols], cells_f32[:, cols])
             nc.tensor.matmul(keys_ps[:, 0:width], weights[:, 0:C], cells[:, cols], start=True, stop=True)
             if width < WIDE:
@@ -73,7 +73,7 @@ def tile_asc_gridcrossattention_kernel(tc, xkv, wkv, bv, q, offs, out):
             else:
                 nc.scalar.copy(keys[:, cols], keys_ps[:, 0:width])
         for cols, width in zip(CHUNKS, CHUNK_WIDTHS):
-            values_ps = psum.tile([C, WIDE], F32, name="values_ps", tag="bank", bufs=5)
+            values_ps = psum.tile([C, WIDE], F32, name="values_ps", tag="bank", bufs=7)
             nc.tensor.matmul(values_ps[:, 0:width], weights[:, C : 2 * C], cells[:, cols], start=True, stop=True)
             nc.scalar.activation(values[:, cols], values_ps[:, 0:width], ACT.Identity, bias=value_bias[:])
 
@@ -102,7 +102,7 @@ def tile_asc_gridcrossattention_kernel(tc, xkv, wkv, bv, q, offs, out):
         besides = [products[1][:], stores[0][:, NEIGHBOURS:, :]]
 
         def new_scores():
-            return psum.tile([BLOCK, NEIGHBOURS, BLOCKS, HEADS], F32, name="scores_ps", bufs=1)
+            return psum.tile([BLOCK, NEIGHBOURS, BLOCKS, HEADS], F32, name="scores_ps", tag="in_turn", bufs=1)
 
         def score(half, n, scores_ps):
             prod = products[half][:, n, :]
@@ -110,7 +110,7 @@ def tile_asc_gridcrossattention_kernel(tc, xkv, wkv, bv, q, offs, out):
                 prod, keys[:].indirect(piece(n, half)), queries[:, half * HALF : (half + 1) * HALF], ALU.mult
             )
             if n < NEIGHBOURS - 1:
-                prod_bf = next_place()[:, HALF // 2 : HALF].rearrange("c (b t) -> c b t", b=BLOCKS).bitcast(BF16)
+                prod_bf = ring.tile([C, BLOCKS, BLOCK], BF16, name="prod_bf")[:, :, :]
             else:
                 prod_bf = across_twice(besides[half], 2)
             nc.scalar.copy(prod_bf, prod.rearrange("c (b t) -> c b t", b=BLOCKS))
@@ -154,7 +154,7 @@ def tile_asc_gridcrossattention_kernel(tc, xkv, wkv, bv, q, offs, out):
                 .unsqueeze(2)
                 .to_broadcast([BLOCK, BLOCKS * HEADS, HEAD_DIM]),
             )
-            attn_ps = psum.tile([C, HALF], F32, name="attn_ps", tag="bank", bufs=5)
+            attn_ps = psum.tile([C, HALF], F32, name="attn_ps", tag="bank", bufs=7)
             for b in range(BLOCKS):
                 block = slice(b * BLOCK, (b + 1) * BLOCK)
                 nc.tensor.transpose(attn_ps[:, block], wide[:, block], identity[:])
@@ -169,23 +169,23 @@ def tile_asc_gridcrossattention_kernel(tc, xkv, wkv, bv, q, offs, out):
         def add_up(half, n, sums_ps, last):
             for b in range(BLOCKS):
                 nc.tensor.matmul(
-                    sums_ps[b][:],
+                    sums_ps[:, b, :],
                     stores[half][:, NEIGHBOURS + n, b * BLOCK : (b + 1) * BLOCK],
                     identity[:],
                     is_transpose=True,
-                    start=(n == 0),
-                    stop=(n == last),
+                    start=(n == 0 and b == 0),
+                    stop=(n == last and b == BLOCKS - 1),
                 )
 
         def new_sums():
-            return [psum.tile([BLOCK, C], F32, name=f"sum_ps{b}", bufs=1) for b in range(BLOCKS)]
+            return psum.tile([BLOCK, BLOCKS, C], F32, name="sums_ps", tag="in_turn", bufs=1)
 
         def finish(half, sums_ps, vector_closes):
             weighted = stores[half][:, NEIGHBOURS:, :]
             sums = per_half.tile([BLOCK, BLOCKS, C], F32, name="sums")
-            out_ps = psum.tile([C, HALF], F32, name="out_ps", tag="bank", bufs=5)
+            out_ps = psum.tile([C, HALF], F32, name="out_ps", tag="bank", bufs=7)
             for b in range(BLOCKS):
-                nc.scalar.copy(sums[:, b, :], sums_ps[b][:])
+                nc.scalar.copy(sums[:, b, :], sums_ps[:, b, :])
                 nc.tensor.transpose(out_ps[:, b * BLOCK : (b + 1) * BLOCK], sums[:, b, :], identity[:])
             result = per_half.tile([C, HALF], F32, name="result")
             if vector_closes:
@@ -222,18 +222,15 @@ def tile_asc_gridcrossattention_kernel(tc, xkv, wkv, bv, q, offs, out):
             weigh(0, n)
             if n + AHEAD < NEIGHBOURS:
                 turn(0, n + AHEAD, attn_0)
-            add_up(0, n - AHEAD, sums_0, last)
         for n in range(AHEAD):
             turn(1, n, attn_1)
-        for n in range(AHEAD):
-            weigh(1, n)
-            turn(1, n + AHEAD, attn_1)
-            add_up(0, NEIGHBOURS - AHEAD + n, sums_0, last)
-        finish(0, sums_0, vector_closes=False)
-        sums_1 = new_sums()
-        for n in range(AHEAD, NEIGHBOURS):
+        for n in range(NEIGHBOURS):
             weigh(1, n)
             if n + AHEAD < NEIGHBOURS:
                 turn(1, n + AHEAD, attn_1)
-            add_up(1, n - AHEAD, sums_1, last - 2)
+            add_up(0, n, sums_0, last)
+        finish(0, sums_0, vector_closes=False)
+        sums_1 = new_sums()
+        for n in range(last - 1):
+            add_up(1, n, sums_1, last - 2)
         finish(1, sums_1, vector_closes=True)

@@ -132,22 +132,24 @@ def tile_asc_gridcrossattention_kernel(tc, xkv, wkv, bv, q, offs, out):
             def for_each_neighbour(values_bh):
                 return values_bh.unsqueeze(1).to_broadcast(whole)
 
-            shifted, total, expd = large(4), small(6), large(7)
-            inverse = per_half.tile([BLOCK, BLOCKS, HEADS], F32, name="inverse")
+            shifted, inverse, expd = large(4), small(6), large(7)
+            total = per_half.tile([BLOCK, BLOCKS, HEADS], F32, name="total")
             nc.vector.tensor_reduce(top, neighbours_last(scores_ps[:]), axis=AXIS.X, op=ALU.max)
             nc.vector.tensor_tensor(shifted, scores_ps[:], for_each_neighbour(top), ALU.subtract)
             nc.scalar.activation(expd, shifted, ACT.Exp, scale=1.0 / math.sqrt(HEAD_DIM))
-            nc.vector.tensor_reduce(total, neighbours_last(expd), axis=AXIS.X, op=ALU.add)
-            nc.vector.reciprocal(inverse[:], total)
+            nc.vector.tensor_reduce(total[:], neighbours_last(expd), axis=AXIS.X, op=ALU.add)
+            nc.vector.reciprocal(inverse, total[:])
             attn_t = per_half.tile(whole, F32, name="attn_t")
-            nc.vector.tensor_tensor(attn_t[:], expd, for_each_neighbour(inverse[:]), ALU.mult)
+            nc.vector.tensor_tensor(attn_t[:], expd, for_each_neighbour(inverse), ALU.mult)
             return attn_t
 
         turned = {}
 
         def turn(half, n, attn_t):
+            by_vector = half == 0 and n < AHEAD
+            spread = nc.vector.tensor_copy if by_vector else nc.scalar.copy
             wide = next_place()
-            nc.scalar.copy(
+            spread(
                 wide.rearrange("t (b h l) -> t (b h) l", b=BLOCKS, l=HEAD_DIM),
                 attn_t[:, n, :, :]
                 .rearrange("t b h -> t (b h)")
@@ -162,8 +164,7 @@ def tile_asc_gridcrossattention_kernel(tc, xkv, wkv, bv, q, offs, out):
 
         def weigh(half, n):
             attn = stores[half][:, n, :]
-            bring = nc.vector.tensor_copy if (half, n) == (0, 0) else nc.scalar.copy
-            bring(attn, turned[half, n][:])
+            nc.scalar.copy(attn, turned[half, n][:])
             nc.vector.tensor_tensor(stores[half][:, NEIGHBOURS + n, :], values[:].indirect(piece(n, half)), attn, ALU.mult)
 
         def add_up(half, n, sums_ps, last):

@@ -16,6 +16,7 @@ HEADS = 4
 HEAD_DIM = 32
 HALF = 256
 PLACES = 3
+LAG = 4
 AHEAD = 2
 HALVES = QUERIES // HALF
 BLOCK = 128
@@ -65,7 +66,7 @@ def tile_asc_gridcrossattention_kernel(tc, xkv, wkv, bv, q, offs, out):
         keys = held.tile([C, CELLS], F32, name="keys")
         values = held.tile([C, CELLS], F32, name="values")
         for cols, width in zip(CHUNKS, CHUNK_WIDTHS):
-            keys_ps = psum.tile([C, WIDE], F32, name="keys_ps", tag="bank", bufs=7)
+            keys_ps = psum.tile([C, WIDE], F32, name="keys_ps", tag="bank", bufs=6)
             nc.vector.tensor_copy(cells[:, cols], cells_f32[:, cols])
             nc.tensor.matmul(keys_ps[:, 0:width], weights[:, 0:C], cells[:, cols], start=True, stop=True)
             if width < WIDE:
@@ -73,7 +74,7 @@ def tile_asc_gridcrossattention_kernel(tc, xkv, wkv, bv, q, offs, out):
             else:
                 nc.scalar.copy(keys[:, cols], keys_ps[:, 0:width])
         for cols, width in zip(CHUNKS, CHUNK_WIDTHS):
-            values_ps = psum.tile([C, WIDE], F32, name="values_ps", tag="bank", bufs=7)
+            values_ps = psum.tile([C, WIDE], F32, name="values_ps", tag="bank", bufs=6)
             nc.tensor.matmul(values_ps[:, 0:width], weights[:, C : 2 * C], cells[:, cols], start=True, stop=True)
             nc.scalar.activation(values[:, cols], values_ps[:, 0:width], ACT.Identity, bias=value_bias[:])
 
@@ -156,7 +157,7 @@ def tile_asc_gridcrossattention_kernel(tc, xkv, wkv, bv, q, offs, out):
                 .unsqueeze(2)
                 .to_broadcast([BLOCK, BLOCKS * HEADS, HEAD_DIM]),
             )
-            attn_ps = psum.tile([C, HALF], F32, name="attn_ps", tag="bank", bufs=7)
+            attn_ps = psum.tile([C, HALF], F32, name="attn_ps", tag="bank", bufs=6)
             for b in range(BLOCKS):
                 block = slice(b * BLOCK, (b + 1) * BLOCK)
                 nc.tensor.transpose(attn_ps[:, block], wide[:, block], identity[:])
@@ -178,13 +179,13 @@ def tile_asc_gridcrossattention_kernel(tc, xkv, wkv, bv, q, offs, out):
                     stop=(n == last and b == BLOCKS - 1),
                 )
 
-        def new_sums():
-            return psum.tile([BLOCK, BLOCKS, C], F32, name="sums_ps", tag="in_turn", bufs=1)
+        def new_sums(tag):
+            return psum.tile([BLOCK, BLOCKS, C], F32, name="sums_ps", tag=tag, bufs=1)
 
         def finish(half, sums_ps, vector_closes):
             weighted = stores[half][:, NEIGHBOURS:, :]
             sums = per_half.tile([BLOCK, BLOCKS, C], F32, name="sums")
-            out_ps = psum.tile([C, HALF], F32, name="out_ps", tag="bank", bufs=7)
+            out_ps = psum.tile([C, HALF], F32, name="out_ps", tag="bank", bufs=6)
             for b in range(BLOCKS):
                 nc.scalar.copy(sums[:, b, :], sums_ps[:, b, :])
                 nc.tensor.transpose(out_ps[:, b * BLOCK : (b + 1) * BLOCK], sums[:, b, :], identity[:])
@@ -213,7 +214,7 @@ def tile_asc_gridcrossattention_kernel(tc, xkv, wkv, bv, q, offs, out):
         for n in range(AHEAD):
             turn(0, n, attn_0)
         score(1, NEIGHBOURS - AHEAD - 1, scores_1)
-        sums_0 = new_sums()
+        sums_0 = new_sums("in_turn")
         for n in range(AHEAD):
             weigh(0, n)
             score(1, NEIGHBOURS - AHEAD + n, scores_1)
@@ -223,15 +224,22 @@ def tile_asc_gridcrossattention_kernel(tc, xkv, wkv, bv, q, offs, out):
             weigh(0, n)
             if n + AHEAD < NEIGHBOURS:
                 turn(0, n + AHEAD, attn_0)
+            if n >= LAG:
+                add_up(0, n - LAG, sums_0, last)
         for n in range(AHEAD):
             turn(1, n, attn_1)
+        sums_1 = new_sums("sums_1")
+        last_1 = last - 2
         for n in range(NEIGHBOURS):
             weigh(1, n)
             if n + AHEAD < NEIGHBOURS:
                 turn(1, n + AHEAD, attn_1)
-            add_up(0, n, sums_0, last)
-        finish(0, sums_0, vector_closes=False)
-        sums_1 = new_sums()
-        for n in range(last - 1):
-            add_up(1, n, sums_1, last - 2)
+            if n < LAG:
+                add_up(0, NEIGHBOURS - LAG + n, sums_0, last)
+            else:
+                add_up(1, n - LAG, sums_1, last_1)
+            if n == LAG:
+                finish(0, sums_0, vector_closes=False)
+        for n in range(NEIGHBOURS - LAG, last_1 + 1):
+            add_up(1, n, sums_1, last_1)
         finish(1, sums_1, vector_closes=True)

@@ -191,9 +191,15 @@ def tile_asc_gridcrossattention_kernel(tc, xkv, wkv, bv, q, offs, out):
                 nc.tensor.transpose(out_ps[:, b * BLOCK : (b + 1) * BLOCK], sums[:, b, :], identity[:])
             result = per_half.tile([C, HALF], F32, name="result")
             if vector_closes:
-                last_two = per_half.tile([C, HALF], F32, name="last_two")
-                nc.vector.tensor_tensor(last_two[:], weighted[:, NEIGHBOURS - 2, :], weighted[:, NEIGHBOURS - 1, :], ALU.add)
-                nc.vector.tensor_tensor(result[:], out_ps[:], last_two[:], ALU.add)
+                blocks = [slice(b * BLOCK, (b + 1) * BLOCK) for b in range(BLOCKS)]
+                two = per_half.tile([C, HALF], F32, name="two")
+                three = per_half.tile([C, HALF], F32, name="three")
+                for block in blocks:
+                    nc.vector.tensor_tensor(two[:, block], weighted[:, NEIGHBOURS - 3, block], weighted[:, NEIGHBOURS - 2, block], ALU.add)
+                for block in blocks:
+                    nc.vector.tensor_tensor(three[:, block], two[:, block], weighted[:, NEIGHBOURS - 1, block], ALU.add)
+                for block in blocks:
+                    nc.vector.tensor_tensor(result[:, block], out_ps[:, block], three[:, block], ALU.add)
             else:
                 nc.scalar.copy(result[:], out_ps[:])
             nc.sync.dma_start(out[:, half * HALF : (half + 1) * HALF], result[:])
@@ -229,7 +235,7 @@ def tile_asc_gridcrossattention_kernel(tc, xkv, wkv, bv, q, offs, out):
         for n in range(AHEAD):
             turn(1, n, attn_1)
         sums_1 = new_sums("sums_1")
-        last_1 = last - 2
+        last_1 = last - 3
         for n in range(NEIGHBOURS):
             weigh(1, n)
             if n + AHEAD < NEIGHBOURS:

@@ -21,6 +21,7 @@ AHEAD = 2
 HALVES = QUERIES // HALF
 BLOCK = 128
 BLOCKS = HALF // BLOCK
+GROUPS = BLOCKS * HEADS
 CHUNK_WIDTHS = [256, 256, 256, 128, 128]
 CHUNKS = [slice(sum(CHUNK_WIDTHS[:j]), sum(CHUNK_WIDTHS[: j + 1])) for j in range(len(CHUNK_WIDTHS))]
 WIDE = max(CHUNK_WIDTHS)
@@ -103,7 +104,7 @@ def tile_asc_gridcrossattention_kernel(tc, xkv, wkv, bv, q, offs, out):
         besides = [products[1][:], stores[0][:, NEIGHBOURS:, :]]
 
         def new_scores():
-            return psum.tile([BLOCK, NEIGHBOURS, BLOCKS, HEADS], F32, name="scores_ps", tag="in_turn", bufs=1)
+            return psum.tile([BLOCK, BLOCKS, HEADS, NEIGHBOURS], F32, name="scores_ps", tag="in_turn", bufs=1)
 
         def score(half, n, scores_ps):
             prod = products[half][:, n, :]
@@ -116,29 +117,27 @@ def tile_asc_gridcrossattention_kernel(tc, xkv, wkv, bv, q, offs, out):
                 prod_bf = across_twice(besides[half], 2)
             nc.scalar.copy(prod_bf, prod.rearrange("c (b t) -> c b t", b=BLOCKS))
             for b in reversed(range(BLOCKS)):
-                nc.tensor.matmul(scores_ps[:, n, b, :], prod_bf[:, b, :], head_cols[:], start=True, stop=True)
+                nc.tensor.matmul(scores_ps[:, b, :, n], prod_bf[:, b, :], head_cols[:], start=True, stop=True)
 
         def softmax_of(scores_ps, beside, top):
-            whole = [BLOCK, NEIGHBOURS, BLOCKS, HEADS]
-
-            def neighbours_last(values):
-                return values.rearrange("t n b h -> t b h n")
+            whole = [BLOCK, GROUPS, NEIGHBOURS]
 
             def small(n):
-                return beside[:, n, 0 : BLOCKS * HEADS].rearrange("t (b h) -> t b h", h=HEADS)
+                return beside[:, n, 0:GROUPS]
 
             def large(n):
-                return across(beside, n, NEIGHBOURS * BLOCKS * HEADS).rearrange("t (n b h) -> t n b h", b=BLOCKS, h=HEADS)
+                return across(beside, n, GROUPS * NEIGHBOURS).rearrange("t (g n) -> t g n", n=NEIGHBOURS)
 
-            def for_each_neighbour(values_bh):
-                return values_bh.unsqueeze(1).to_broadcast(whole)
+            def for_each_neighbour(values):
+                return values.unsqueeze(2).to_broadcast(whole)
 
+            scores = scores_ps[:].rearrange("t b h n -> t (b h) n")
             shifted, inverse, expd = large(4), small(6), large(7)
-            total = per_half.tile([BLOCK, BLOCKS, HEADS], F32, name="total")
-            nc.vector.tensor_reduce(top, neighbours_last(scores_ps[:]), axis=AXIS.X, op=ALU.max)
-            nc.vector.tensor_tensor(shifted, scores_ps[:], for_each_neighbour(top), ALU.subtract)
+            total = per_half.tile([BLOCK, GROUPS], F32, name="total")
+            nc.vector.tensor_reduce(top, scores, axis=AXIS.X, op=ALU.max)
+            nc.vector.tensor_tensor(shifted, scores, for_each_neighbour(top), ALU.subtract)
             nc.scalar.activation(expd, shifted, ACT.Exp, scale=1.0 / math.sqrt(HEAD_DIM))
-            nc.vector.tensor_reduce(total[:], neighbours_last(expd), axis=AXIS.X, op=ALU.add)
+            nc.vector.tensor_reduce(total[:], expd, axis=AXIS.X, op=ALU.add)
             nc.vector.reciprocal(inverse, total[:])
             attn_t = per_half.tile(whole, F32, name="attn_t")
             nc.vector.tensor_tensor(attn_t[:], expd, for_each_neighbour(inverse), ALU.mult)
@@ -151,11 +150,8 @@ def tile_asc_gridcrossattention_kernel(tc, xkv, wkv, bv, q, offs, out):
             spread = nc.vector.tensor_copy if by_vector else nc.scalar.copy
             wide = next_place()
             spread(
-                wide.rearrange("t (b h l) -> t (b h) l", b=BLOCKS, l=HEAD_DIM),
-                attn_t[:, n, :, :]
-                .rearrange("t b h -> t (b h)")
-                .unsqueeze(2)
-                .to_broadcast([BLOCK, BLOCKS * HEADS, HEAD_DIM]),
+                wide.rearrange("t (g l) -> t g l", l=HEAD_DIM),
+                attn_t[:, :, n].unsqueeze(2).to_broadcast([BLOCK, GROUPS, HEAD_DIM]),
             )
             attn_ps = psum.tile([C, HALF], F32, name="attn_ps", tag="bank", bufs=6)
             for b in range(BLOCKS):
@@ -204,11 +200,7 @@ def tile_asc_gridcrossattention_kernel(tc, xkv, wkv, bv, q, offs, out):
                 nc.scalar.copy(result[:], out_ps[:])
             nc.sync.dma_start(out[:, half * HALF : (half + 1) * HALF], result[:])
 
-        tops = [
-            held.tile([BLOCK, BLOCKS * HEADS], F32, name="top")[:, 0 : BLOCKS * HEADS],
-            stores[0][:, 0, 0 : BLOCKS * HEADS],
-        ]
-        tops = [top.rearrange("t (b h) -> t b h", h=HEADS) for top in tops]
+        tops = [held.tile([BLOCK, GROUPS], F32, name="top")[:, :], stores[0][:, 0, 0:GROUPS]]
         last = NEIGHBOURS - 1
         scores_0 = new_scores()
         for n in range(NEIGHBOURS):

@@ -182,20 +182,28 @@ def tile_asc_gridcrossattention_kernel(tc, xkv, wkv, bv, q, offs, out):
             weighted = stores[half][:, NEIGHBOURS:, :]
             sums = per_half.tile([BLOCK, BLOCKS, C], F32, name="sums")
             out_ps = psum.tile([C, HALF], F32, name="out_ps", tag="bank", bufs=6)
+            if vector_closes:
+                nc.tensor.matmul(out_ps[:], identity[:], weighted[:, NEIGHBOURS - 3, :], start=True, stop=False)
             for b in range(BLOCKS):
                 nc.scalar.copy(sums[:, b, :], sums_ps[:, b, :])
-                nc.tensor.transpose(out_ps[:, b * BLOCK : (b + 1) * BLOCK], sums[:, b, :], identity[:])
+                nc.tensor.matmul(
+                    out_ps[:, b * BLOCK : (b + 1) * BLOCK],
+                    sums[:, b, :],
+                    identity[:],
+                    is_transpose=True,
+                    start=not vector_closes,
+                    stop=not vector_closes or b == BLOCKS - 1,
+                )
             result = per_half.tile([C, HALF], F32, name="result")
             if vector_closes:
                 blocks = [slice(b * BLOCK, (b + 1) * BLOCK) for b in range(BLOCKS)]
                 two = per_half.tile([C, HALF], F32, name="two")
-                three = per_half.tile([C, HALF], F32, name="three")
                 for block in blocks:
-                    nc.vector.tensor_tensor(two[:, block], weighted[:, NEIGHBOURS - 3, block], weighted[:, NEIGHBOURS - 2, block], ALU.add)
+                    nc.vector.tensor_tensor(
+                        two[:, block], weighted[:, NEIGHBOURS - 2, block], weighted[:, NEIGHBOURS - 1, block], ALU.add
+                    )
                 for block in blocks:
-                    nc.vector.tensor_tensor(three[:, block], two[:, block], weighted[:, NEIGHBOURS - 1, block], ALU.add)
-                for block in blocks:
-                    nc.vector.tensor_tensor(result[:, block], out_ps[:, block], three[:, block], ALU.add)
+                    nc.vector.tensor_tensor(result[:, block], out_ps[:, block], two[:, block], ALU.add)
             else:
                 nc.scalar.copy(result[:], out_ps[:])
             nc.sync.dma_start(out[:, half * HALF : (half + 1) * HALF], result[:])

@@ -178,12 +178,11 @@ def tile_asc_gridcrossattention_kernel(tc, xkv, wkv, bv, q, offs, out):
         def new_sums(tag):
             return psum.tile([BLOCK, BLOCKS, C], F32, name="sums_ps", tag=tag, bufs=1)
 
-        def finish(half, sums_ps, vector_closes):
-            weighted = stores[half][:, NEIGHBOURS:, :]
-            sums = per_half.tile([BLOCK, BLOCKS, C], F32, name="sums")
+        def turn_back(sums_ps, straight=None):
             out_ps = psum.tile([C, HALF], F32, name="out_ps", tag="bank", bufs=6)
-            if vector_closes:
-                nc.tensor.matmul(out_ps[:], identity[:], weighted[:, NEIGHBOURS - 3, :], start=True, stop=False)
+            if straight is not None:
+                nc.tensor.matmul(out_ps[:], identity[:], straight, start=True, stop=False)
+            sums = per_half.tile([BLOCK, BLOCKS, C], F32, name="sums")
             for b in range(BLOCKS):
                 nc.scalar.copy(sums[:, b, :], sums_ps[:, b, :])
                 nc.tensor.matmul(
@@ -191,21 +190,12 @@ def tile_asc_gridcrossattention_kernel(tc, xkv, wkv, bv, q, offs, out):
                     sums[:, b, :],
                     identity[:],
                     is_transpose=True,
-                    start=not vector_closes,
-                    stop=not vector_closes or b == BLOCKS - 1,
+                    start=straight is None,
+                    stop=straight is None or b == BLOCKS - 1,
                 )
-            result = per_half.tile([C, HALF], F32, name="result")
-            if vector_closes:
-                blocks = [slice(b * BLOCK, (b + 1) * BLOCK) for b in range(BLOCKS)]
-                two = per_half.tile([C, HALF], F32, name="two")
-                for block in blocks:
-                    nc.vector.tensor_tensor(
-                        two[:, block], weighted[:, NEIGHBOURS - 2, block], weighted[:, NEIGHBOURS - 1, block], ALU.add
-                    )
-                for block in blocks:
-                    nc.vector.tensor_tensor(result[:, block], out_ps[:, block], two[:, block], ALU.add)
-            else:
-                nc.scalar.copy(result[:], out_ps[:])
+            return out_ps
+
+        def store(half, result):
             nc.sync.dma_start(out[:, half * HALF : (half + 1) * HALF], result[:])
 
         tops = [held.tile([BLOCK, GROUPS], F32, name="top")[:, :], stores[0][:, 0, 0:GROUPS]]
@@ -245,7 +235,20 @@ def tile_asc_gridcrossattention_kernel(tc, xkv, wkv, bv, q, offs, out):
             else:
                 add_up(1, n - LAG, sums_1, last_1)
             if n == LAG:
-                finish(0, sums_0, vector_closes=False)
+                out_ps_0 = turn_back(sums_0)
+            if n == LAG + AHEAD:
+                result_0 = held.tile([C, HALF], F32, name="result_0")
+                nc.scalar.copy(result_0[:], out_ps_0[:])
+                store(0, result_0)
         for n in range(NEIGHBOURS - LAG, last_1 + 1):
             add_up(1, n, sums_1, last_1)
-        finish(1, sums_1, vector_closes=True)
+        weighted = stores[1][:, NEIGHBOURS:, :]
+        out_ps_1 = turn_back(sums_1, straight=weighted[:, last - 2, :])
+        result_1 = held.tile([C, HALF], F32, name="result_1")
+        two = held.tile([C, HALF], F32, name="two")
+        blocks = [slice(b * BLOCK, (b + 1) * BLOCK) for b in range(BLOCKS)]
+        for block in blocks:
+            nc.vector.tensor_tensor(two[:, block], weighted[:, last - 1, block], weighted[:, last, block], ALU.add)
+        for block in blocks:
+            nc.vector.tensor_tensor(result_1[:, block], out_ps_1[:, block], two[:, block], ALU.add)
+        store(1, result_1)

import math

import concourse.mybir as mybir
from concourse.masks import make_identity

F32, BF16, U16 = mybir.dt.float32, mybir.dt.bfloat16, mybir.dt.uint16
ALU = mybir.AluOpType
ACT = mybir.ActivationFunctionType
AXIS = mybir.AxisListType

C = 128
CELLS = 1024
QUERIES = 512
NEIGHBOURS = 9
HEADS = 4
HEAD_DIM = 32
HALF = 256
PLACES = 3
LAG = 4
AHEAD = 2
HALVES = QUERIES // HALF
BLOCK = 128
BLOCKS = HALF // BLOCK
GROUPS = BLOCKS * HEADS
CHUNK_WIDTHS = [256, 256, 256, 128, 128]
CHUNKS = [slice(sum(CHUNK_WIDTHS[:j]), sum(CHUNK_WIDTHS[: j + 1])) for j in range(len(CHUNK_WIDTHS))]
WIDE = max(CHUNK_WIDTHS)

FLOPS = 2 * C * (2 * C) * CELLS + 4 * C * NEIGHBOURS * QUERIES


def tile_asc_gridcrossattention_kernel(tc, xkv, wkv, bv, q, offs, out):
    nc = tc.nc
    with (
        tc.tile_pool(name="held", bufs=1) as held,
        tc.tile_pool(name="ring", bufs=4) as ring,
        tc.tile_pool(name="per_half", bufs=HALVES) as per_half,
        tc.psum_pool(name="psum", bufs=2) as psum,
    ):
        weights = held.tile([C, 2 * C], BF16, name="weights")
        nc.scalar.dma_start(weights[:], wkv)
        cells_f32 = held.tile([C, CELLS], F32, name="cells_f32")
        for j, cols in enumerate(CHUNKS):
            queue = nc.sync if j % 2 == 0 else nc.scalar
            queue.dma_start(cells_f32[:, cols], xkv[:, cols])
        offsets = held.tile([C, NEIGHBOURS * QUERIES // 16], U16, name="offsets")
        nc.sync.dma_start(offsets[:], offs)
        queries = held.tile([C, QUERIES], F32, name="queries")
        for half in range(HALVES):
            cols = slice(half * HALF, (half + 1) * HALF)
            nc.sync.dma_start(queries[:, cols], q[:, cols])
        value_bias = held.tile([C, 1], F32, name="value_bias")
        nc.sync.dma_start(value_bias[:], bv)

        warm = held.tile([C, 1], F32, name="warm")
        nc.gpsimd.memset(warm[:], 0.0)
        warmed = held.tile([C, 1], F32, name="warmed")
        nc.scalar.activation(warmed[:], warm[:], ACT.Exp)
        head_cols = held.tile([C, HEADS], BF16, name="head_cols")
        nc.vector.memset(head_cols[:], 0.0)
        for h in range(HEADS):
            nc.vector.memset(head_cols[h * HEAD_DIM : (h + 1) * HEAD_DIM, h : h + 1], 1.0)
        identity = held.tile([C, C], F32, name="identity")
        make_identity(nc, identity[:])

        cells = held.tile([C, CELLS], BF16, name="cells")
        keys = held.tile([C, CELLS], F32, name="keys")
        values = held.tile([C, CELLS], F32, name="values")
        for cols, width in zip(CHUNKS, CHUNK_WIDTHS):
            keys_ps = psum.tile([C, WIDE], F32, name="keys_ps", tag="bank", bufs=6)
            nc.vector.tensor_copy(cells[:, cols], cells_f32[:, cols])
            nc.tensor.matmul(keys_ps[:, 0:width], weights[:, 0:C], cells[:, cols], start=True, stop=True)
            if width < WIDE:
                nc.vector.tensor_copy(keys[:, cols], keys_ps[:, 0:width])
            else:
                nc.scalar.copy(keys[:, cols], keys_ps[:, 0:width])
        for cols, width in zip(CHUNKS, CHUNK_WIDTHS):
            values_ps = psum.tile([C, WIDE], F32, name="values_ps", tag="bank", bufs=6)
            nc.tensor.matmul(values_ps[:, 0:width], weights[:, C : 2 * C], cells[:, cols], start=True, stop=True)
            nc.scalar.activation(values[:, cols], values_ps[:, 0:width], ACT.Identity, bias=value_bias[:])

        def piece(n, half):
            first = (n * QUERIES + half * HALF) // 16
            return offsets[:, first : first + HALF // 16]

        products = [held.tile([C, NEIGHBOURS, HALF], F32, name=f"products{half}") for half in range(HALVES)]
        stores = [held.tile([C, 2 * NEIGHBOURS, HALF], F32, name=f"store{half}") for half in range(HALVES)]
        staged = held.tile([C, PLACES, HALF], F32, name="staged")
        taken = []

        def next_place():
            taken.append(len(taken) % PLACES)
            return staged[:, taken[-1], :]

        def across(places, n, width):
            border = (n + 1) * HALF
            return places.rearrange("c n t -> c (n t)")[:, border - width // 2 : border + width // 2]

        def across_twice(places, n):
            border = (n + 1) * HALF
            run = places.rearrange("c n t -> c (n t)")[:, border - BLOCK // 4 : border - BLOCK // 4 + 2 * BLOCKS * HALF]
            return run.rearrange("c (b t) -> c b t", b=BLOCKS)[:, :, 0 : BLOCK // 2].bitcast(BF16)

        besides = [products[1][:], stores[0][:, NEIGHBOURS:, :]]

        def new_scores():
            return psum.tile([BLOCK, BLOCKS, HEADS, NEIGHBOURS], F32, name="scores_ps", tag="in_turn", bufs=1)

        def score(half, n, scores_ps):
            prod = products[half][:, n, :]
            nc.vector.tensor_tensor(
                prod, keys[:].indirect(piece(n, half)), queries[:, half * HALF : (half + 1) * HALF], ALU.mult
            )
            if n < NEIGHBOURS - 1:
                prod_bf = ring.tile([C, BLOCKS, BLOCK], BF16, name="prod_bf")[:, :, :]
            else:
                prod_bf = across_twice(besides[half], 2)
            nc.scalar.copy(prod_bf, prod.rearrange("c (b t) -> c b t", b=BLOCKS))
            for b in reversed(range(BLOCKS)):
                nc.tensor.matmul(scores_ps[:, b, :, n], prod_bf[:, b, :], head_cols[:], start=True, stop=True)

        def softmax_of(scores_ps, beside, top):
            whole = [BLOCK, GROUPS, NEIGHBOURS]

            def small(n):
                return beside[:, n, 0:GROUPS]

            def large(n):
                return across(beside, n, GROUPS * NEIGHBOURS).rearrange("t (g n) -> t g n", n=NEIGHBOURS)

            def for_each_neighbour(values):
                return values.unsqueeze(2).to_broadcast(whole)

            scores = scores_ps[:].rearrange("t b h n -> t (b h) n")
            shifted, inverse, expd = large(4), small(6), large(7)
            total = per_half.tile([BLOCK, GROUPS], F32, name="total")
            nc.vector.tensor_reduce(top, scores, axis=AXIS.X, op=ALU.max)
            nc.vector.tensor_tensor(shifted, scores, for_each_neighbour(top), ALU.subtract)
            nc.scalar.activation(expd, shifted, ACT.Exp, scale=1.0 / math.sqrt(HEAD_DIM))
            nc.vector.tensor_reduce(total[:], expd, axis=AXIS.X, op=ALU.add)
            nc.vector.reciprocal(inverse, total[:])
            attn_t = per_half.tile(whole, F32, name="attn_t")
            nc.vector.tensor_tensor(attn_t[:], expd, for_each_neighbour(inverse), ALU.mult)
            return attn_t

        turned = {}

        def turn(half, n, attn_t):
            by_vector = half == 0 and n < AHEAD
            spread = nc.vector.tensor_copy if by_vector else nc.scalar.copy
            wide = next_place()
            spread(
                wide.rearrange("t (g l) -> t g l", l=HEAD_DIM),
                attn_t[:, :, n].unsqueeze(2).to_broadcast([BLOCK, GROUPS, HEAD_DIM]),
            )
            attn_ps = psum.tile([C, HALF], F32, name="attn_ps", tag="bank", bufs=6)
            for b in range(BLOCKS):
                block = slice(b * BLOCK, (b + 1) * BLOCK)
                nc.tensor.transpose(attn_ps[:, block], wide[:, block], identity[:])
            turned[half, n] = attn_ps

        def weigh(half, n):
            attn = stores[half][:, n, :]
            nc.scalar.copy(attn, turned[half, n][:])
            nc.vector.tensor_tensor(stores[half][:, NEIGHBOURS + n, :], values[:].indirect(piece(n, half)), attn, ALU.mult)

        def add_up(half, n, sums_ps, last):
            for b in range(BLOCKS):
                nc.tensor.matmul(
                    sums_ps[:, b, :],
                    stores[half][:, NEIGHBOURS + n, b * BLOCK : (b + 1) * BLOCK],
                    identity[:],
                    is_transpose=True,
                    start=(n == 0 and b == 0),
                    stop=(n == last and b == BLOCKS - 1),
                )

        def new_sums(tag):
            return psum.tile([BLOCK, BLOCKS, C], F32, name="sums_ps", tag=tag, bufs=1)

        def turn_back(sums_ps, straight=None):
            out_ps = psum.tile([C, HALF], F32, name="out_ps", tag="bank", bufs=6)
            if straight is not None:
                nc.tensor.matmul(out_ps[:], identity[:], straight, start=True, stop=False)
            sums = per_half.tile([BLOCK, BLOCKS, C], F32, name="sums")
            for b in range(BLOCKS):
                nc.scalar.copy(sums[:, b, :], sums_ps[:, b, :])
                nc.tensor.matmul(
                    out_ps[:, b * BLOCK : (b + 1) * BLOCK],
                    sums[:, b, :],
                    identity[:],
                    is_transpose=True,
                    start=straight is None,
                    stop=straight is None or b == BLOCKS - 1,
                )
            return out_ps

        def store(half, result):
            nc.sync.dma_start(out[:, half * HALF : (half + 1) * HALF], result[:])

        tops = [held.tile([BLOCK, GROUPS], F32, name="top")[:, :], stores[0][:, 0, 0:GROUPS]]
        last = NEIGHBOURS - 1
        scores_0 = new_scores()
        for n in range(NEIGHBOURS):
            score(0, n, scores_0)
        attn_0 = softmax_of(scores_0, besides[0], tops[0])
        scores_1 = new_scores()
        for n in range(NEIGHBOURS - AHEAD - 1):
            score(1, n, scores_1)
        for n in range(AHEAD):
            turn(0, n, attn_0)
        score(1, NEIGHBOURS - AHEAD - 1, scores_1)
        sums_0 = new_sums("in_turn")
        for n in range(AHEAD):
            weigh(0, n)
            score(1, NEIGHBOURS - AHEAD + n, scores_1)
            turn(0, AHEAD + n, attn_0)
        attn_1 = softmax_of(scores_1, besides[1], tops[1])
        for n in range(AHEAD, NEIGHBOURS):
            weigh(0, n)
            if n + AHEAD < NEIGHBOURS:
                turn(0, n + AHEAD, attn_0)
            if n >= LAG:
                add_up(0, n - LAG, sums_0, last)
        for n in range(AHEAD):
            turn(1, n, attn_1)
        sums_1 = new_sums("sums_1")
        last_1 = last - 3
        for n in range(NEIGHBOURS):
            weigh(1, n)
            if n + AHEAD < NEIGHBOURS:
                turn(1, n + AHEAD, attn_1)
            if n < LAG:
                add_up(0, NEIGHBOURS - LAG + n, sums_0, last)
            else:
                add_up(1, n - LAG, sums_1, last_1)
            if n == LAG:
                out_ps_0 = turn_back(sums_0)
            if n == LAG + AHEAD:
                result_0 = held.tile([C, HALF], F32, name="result_0")
                nc.scalar.copy(result_0[:], out_ps_0[:])
                store(0, result_0)
        for n in range(NEIGHBOURS - LAG, last_1 + 1):
            add_up(1, n, sums_1, last_1)
        weighted = stores[1][:, NEIGHBOURS:, :]
        out_ps_1 = turn_back(sums_1, straight=weighted[:, last - 2, :])
        result_1 = held.tile([C, HALF], F32, name="result_1")
        two = held.tile([C, HALF], F32, name="two")
        blocks = [slice(b * BLOCK, (b + 1) * BLOCK) for b in range(BLOCKS)]
        for block in blocks:
            nc.vector.tensor_tensor(two[:, block], weighted[:, last - 1, block], weighted[:, last, block], ALU.add)
        for block in blocks:
            nc.vector.tensor_tensor(result_1[:, block], out_ps_1[:, block], two[:, block], ALU.add)
        store(1, result_1)
